import numpy as np
import ml_dtypes

BF16 = ml_dtypes.bfloat16


def bf(x):
    return np.asarray(x, np.float32).astype(BF16)


def f32(x):
    return np.asarray(x, np.float32)


def f64(x):
    return np.asarray(x).astype(np.float64)


def striped(idx):
    return np.tile(idx.reshape(-1, 16).T, (8, 1))


S, D, M, T, DEPTH, NPT, N = 256, 128, 128, 256, 3, 7, 1792


def setup_inputs():
    return {"table": bf(np.random.standard_normal((D, S))), "w": bf(np.random.standard_normal((D, M)) / np.sqrt(D)), "b": f32(0.1 * np.random.standard_normal((M, 1))), "offs": striped(np.concatenate([np.random.permutation(S) for _ in range(N // S)]))}


def reference(table, w, b, offs):
    idx = offs[:16].T.reshape(-1)
    e = f64(w).T @ f64(table)[:, idx] + f64(b)
    h = e.reshape(M, NPT, T).copy()
    for level in range(DEPTH - 2, -1, -1):
        start, end = 2**level - 1, 2 ** (level + 1) - 1
        for node in range(start, end):
            h[:, node] = h[:, node] + h[:, 2 * node + 1] + h[:, 2 * node + 2]
    return np.maximum(h.max(axis=1), 0.0)

@@ -1,0 +1,52 @@
+import concourse.mybir as mybir
+
+BF16, F32, U16 = mybir.dt.bfloat16, mybir.dt.float32, mybir.dt.uint16
+ADD, MAX = mybir.AluOpType.add, mybir.AluOpType.max
+
+P = 128
+WORDS = 256
+TREES = 256
+NODES = 7
+FIRST_LEAF = 3
+PIECE_COLS = TREES // 16
+
+FLOPS = 2 * P * P * NODES * TREES
+
+
+def tile_batchprogramclassifier_kernel(tc, table, w, b, offs, out):
+    nc = tc.nc
+    with (
+        tc.tile_pool(name="held", bufs=1) as held,
+        tc.psum_pool(name="psum", bufs=1) as psum,
+    ):
+        offsets = held.tile([P, NODES * PIECE_COLS], U16, name="offsets")
+        nc.sync.dma_start(offsets[:], offs)
+        words = held.tile([P, WORDS], BF16, name="words")
+        nc.scalar.dma_start(words[:], table)
+        weights = held.tile([P, P], BF16, name="weights")
+        nc.sync.dma_start(weights[:], w)
+        bias = held.tile([P, 1], F32, name="bias")
+        nc.scalar.dma_start(bias[:], b)
+
+        projected = []
+        for n in range(NODES):
+            bank = psum.tile([P, TREES], F32, name=f"projected{n}")
+            piece = offsets[:, n * PIECE_COLS : (n + 1) * PIECE_COLS]
+            nc.tensor.matmul(bank[:], weights[:], words[:].indirect(piece), start=True, stop=True)
+            projected.append(bank)
+
+        subtree = [held.tile([P, TREES], F32, name=f"subtree{n}") for n in range(NODES)]
+        for n in reversed(range(NODES)):
+            if n >= FIRST_LEAF:
+                nc.vector.tensor_scalar(subtree[n][:], projected[n][:], bias[:], None, ADD)
+            else:
+                nc.vector.scalar_tensor_tensor(
+                    subtree[n][:], projected[n][:], bias[:], subtree[2 * n + 1][:], ADD, ADD
+                )
+                nc.vector.tensor_tensor(subtree[n][:], subtree[n][:], subtree[2 * n + 2][:], ADD)
+
+        best = held.tile([P, TREES], F32, name="best")
+        nc.vector.tensor_scalar(best[:], subtree[0][:], 0.0, None, MAX)
+        for n in range(1, NODES):
+            nc.vector.tensor_tensor(best[:], best[:], subtree[n][:], MAX)
+        nc.sync.dma_start(out, best[:])

@@ -1,14 +1,16 @@
 import concourse.mybir as mybir
 
 BF16, F32, U16 = mybir.dt.bfloat16, mybir.dt.float32, mybir.dt.uint16
-ADD, MAX = mybir.AluOpType.add, mybir.AluOpType.max
+ADD, MAX, MULT = mybir.AluOpType.add, mybir.AluOpType.max, mybir.AluOpType.mult
+IDENTITY, RELU = mybir.ActivationFunctionType.Identity, mybir.ActivationFunctionType.Relu
 
 P = 128
 WORDS = 256
 TREES = 256
 NODES = 7
-FIRST_LEAF = 3
 PIECE_COLS = TREES // 16
+BANK = 512
+WARM_UP = 5
 
 FLOPS = 2 * P * P * NODES * TREES
 
@@ -28,25 +30,54 @@ def tile_batchprogramclassifier_kernel(tc, table, w, b, offs, out):
         bias = held.tile([P, 1], F32, name="bias")
         nc.scalar.dma_start(bias[:], b)
 
-        projected = []
-        for n in range(NODES):
-            bank = psum.tile([P, TREES], F32, name=f"projected{n}")
-            piece = offsets[:, n * PIECE_COLS : (n + 1) * PIECE_COLS]
-            nc.tensor.matmul(bank[:], weights[:], words[:].indirect(piece), start=True, stop=True)
-            projected.append(bank)
+        zeros = held.tile([P, BANK], BF16, name="zeros")
+        nc.vector.memset(zeros[:], 0.0)
+        unused = psum.tile([P, BANK], F32, name="unused")
+        for _ in range(WARM_UP):
+            nc.tensor.matmul(unused[:], zeros[:, :P], zeros[:], start=True, stop=True)
 
-        subtree = [held.tile([P, TREES], F32, name=f"subtree{n}") for n in range(NODES)]
-        for n in reversed(range(NODES)):
-            if n >= FIRST_LEAF:
-                nc.vector.tensor_scalar(subtree[n][:], projected[n][:], bias[:], None, ADD)
-            else:
-                nc.vector.scalar_tensor_tensor(
-                    subtree[n][:], projected[n][:], bias[:], subtree[2 * n + 1][:], ADD, ADD
-                )
-                nc.vector.tensor_tensor(subtree[n][:], subtree[n][:], subtree[2 * n + 2][:], ADD)
+        bias3 = held.tile([P, 1], F32, name="bias3")
+        nc.vector.tensor_scalar(bias3[:], bias[:], 3.0, None, MULT)
 
-        best = held.tile([P, TREES], F32, name="best")
-        nc.vector.tensor_scalar(best[:], subtree[0][:], 0.0, None, MAX)
-        for n in range(1, NODES):
-            nc.vector.tensor_tensor(best[:], best[:], subtree[n][:], MAX)
-        nc.sync.dma_start(out, best[:])
+        def project_sum(name, nodes):
+            bank = psum.tile([P, TREES], F32, name=name)
+            for n in nodes:
+                first, last = n == nodes[0], n == nodes[-1]
+                cuts = 1 if first or last else 2
+                width = TREES // cuts
+                for c in range(cuts):
+                    col = n * PIECE_COLS + c * (width // 16)
+                    nc.tensor.matmul(
+                        bank[:, c * width : (c + 1) * width],
+                        weights[:],
+                        words[:].indirect(offsets[:, col : col + width // 16]),
+                        start=first,
+                        stop=last,
+                    )
+            return bank
+
+        root = project_sum("root", [0])
+        left = project_sum("left", [1, 3, 4])
+        leaf = {n: project_sum(f"leaf{n}", [n]) for n in (3, 4, 5, 6)}
+        right = project_sum("right", [2, 5, 6])
+
+        root_own = held.tile([P, TREES], F32, name="root_own")
+        nc.scalar.activation(root_own[:], root[:], IDENTITY, bias=bias[:])
+        above = held.tile([P, TREES], F32, name="above")
+        nc.vector.scalar_tensor_tensor(above[:], left[:], bias3[:], root_own[:], ADD, ADD)
+        nc.vector.tensor_scalar(above[:], above[:], 0.0, None, MAX)
+
+        best = {}
+        for side, (scalar_leaf, vector_leaf) in (("a", (3, 4)), ("b", (5, 6))):
+            best[side] = held.tile([P, TREES], F32, name=f"best_{side}")
+            nc.scalar.activation(best[side][:], leaf[scalar_leaf][:], RELU, bias=bias[:])
+            nc.vector.scalar_tensor_tensor(
+                best[side][:], leaf[vector_leaf][:], bias[:], best[side][:], ADD, MAX
+            )
+        nc.vector.scalar_tensor_tensor(best["a"][:], left[:], bias3[:], best["a"][:], ADD, MAX)
+        nc.vector.tensor_tensor(best["a"][:], best["a"][:], best["b"][:], MAX)
+
+        top = held.tile([P, TREES], F32, name="top")
+        nc.vector.scalar_tensor_tensor(top[:], right[:], bias3[:], above[:], ADD, ADD)
+        nc.vector.tensor_tensor(top[:], top[:], best["a"][:], MAX)
+        nc.sync.dma_start(out, top[:])

@@ -10,7 +10,7 @@ TREES = 256
 NODES = 7
 PIECE_COLS = TREES // 16
 BANK = 512
-WARM_UP = 5
+WARM_UP = 3
 
 FLOPS = 2 * P * P * NODES * TREES
 
@@ -30,11 +30,12 @@ def tile_batchprogramclassifier_kernel(tc, table, w, b, offs, out):
         bias = held.tile([P, 1], F32, name="bias")
         nc.scalar.dma_start(bias[:], b)
 
-        zeros = held.tile([P, BANK], BF16, name="zeros")
+        zeros = held.tile([P, P], BF16, name="zeros")
         nc.vector.memset(zeros[:], 0.0)
         unused = psum.tile([P, BANK], F32, name="unused")
-        for _ in range(WARM_UP):
-            nc.tensor.matmul(unused[:], zeros[:, :P], zeros[:], start=True, stop=True)
+        zeros_wide = zeros[:].unsqueeze(1).to_broadcast([P, BANK // P, P])
+        for repeat in range(WARM_UP):
+            nc.tensor.matmul(unused[:], zeros[:], zeros_wide, start=True, stop=True)
 
         bias3 = held.tile([P, 1], F32, name="bias3")
         nc.vector.tensor_scalar(bias3[:], bias[:], 3.0, None, MULT)

@@ -37,6 +37,9 @@ def tile_batchprogramclassifier_kernel(tc, table, w, b, offs, out):
         for repeat in range(WARM_UP):
             nc.tensor.matmul(unused[:], zeros[:], zeros_wide, start=True, stop=True)
 
+        table_loaded = held.tile([P, 1], F32, name="table_loaded")
+        nc.scalar.activation(table_loaded[:], zeros[:, 0:1], RELU)
+
         bias3 = held.tile([P, 1], F32, name="bias3")
         nc.vector.tensor_scalar(bias3[:], bias[:], 3.0, None, MULT)
 

@@ -9,8 +9,6 @@ WORDS = 256
 TREES = 256
 NODES = 7
 PIECE_COLS = TREES // 16
-BANK = 512
-WARM_UP = 3
 
 FLOPS = 2 * P * P * NODES * TREES
 
@@ -30,15 +28,11 @@ def tile_batchprogramclassifier_kernel(tc, table, w, b, offs, out):
         bias = held.tile([P, 1], F32, name="bias")
         nc.scalar.dma_start(bias[:], b)
 
-        zeros = held.tile([P, P], BF16, name="zeros")
+        zeros = held.tile([P, 1], F32, name="zeros")
         nc.vector.memset(zeros[:], 0.0)
-        unused = psum.tile([P, BANK], F32, name="unused")
-        zeros_wide = zeros[:].unsqueeze(1).to_broadcast([P, BANK // P, P])
-        for repeat in range(WARM_UP):
-            nc.tensor.matmul(unused[:], zeros[:], zeros_wide, start=True, stop=True)
 
         table_loaded = held.tile([P, 1], F32, name="table_loaded")
-        nc.scalar.activation(table_loaded[:], zeros[:, 0:1], RELU)
+        nc.scalar.activation(table_loaded[:], zeros[:], RELU)
 
         bias3 = held.tile([P, 1], F32, name="bias3")
         nc.vector.tensor_scalar(bias3[:], bias[:], 3.0, None, MULT)

@@ -2,7 +2,7 @@ import concourse.mybir as mybir
 
 BF16, F32, U16 = mybir.dt.bfloat16, mybir.dt.float32, mybir.dt.uint16
 ADD, MAX, MULT = mybir.AluOpType.add, mybir.AluOpType.max, mybir.AluOpType.mult
-IDENTITY, RELU = mybir.ActivationFunctionType.Identity, mybir.ActivationFunctionType.Relu
+RELU = mybir.ActivationFunctionType.Relu
 
 P = 128
 WORDS = 256
@@ -30,7 +30,6 @@ def tile_batchprogramclassifier_kernel(tc, table, w, b, offs, out):
 
         zeros = held.tile([P, 1], F32, name="zeros")
         nc.vector.memset(zeros[:], 0.0)
-
         table_loaded = held.tile([P, 1], F32, name="table_loaded")
         nc.scalar.activation(table_loaded[:], zeros[:], RELU)
 
@@ -54,28 +53,36 @@ def tile_batchprogramclassifier_kernel(tc, table, w, b, offs, out):
                     )
             return bank
 
-        root = project_sum("root", [0])
-        left = project_sum("left", [1, 3, 4])
-        leaf = {n: project_sum(f"leaf{n}", [n]) for n in (3, 4, 5, 6)}
+        e3 = project_sum("e3", [3])
+        e4 = project_sum("e4", [4])
+        e1 = project_sum("e1", [1])
+        e0 = project_sum("e0", [0])
+        e5 = project_sum("e5", [5])
+        e6 = project_sum("e6", [6])
         right = project_sum("right", [2, 5, 6])
 
-        root_own = held.tile([P, TREES], F32, name="root_own")
-        nc.scalar.activation(root_own[:], root[:], IDENTITY, bias=bias[:])
-        above = held.tile([P, TREES], F32, name="above")
-        nc.vector.scalar_tensor_tensor(above[:], left[:], bias3[:], root_own[:], ADD, ADD)
-        nc.vector.tensor_scalar(above[:], above[:], 0.0, None, MAX)
+        def work(name):
+            return held.tile([P, TREES], F32, name=name)
 
-        best = {}
-        for side, (scalar_leaf, vector_leaf) in (("a", (3, 4)), ("b", (5, 6))):
-            best[side] = held.tile([P, TREES], F32, name=f"best_{side}")
-            nc.scalar.activation(best[side][:], leaf[scalar_leaf][:], RELU, bias=bias[:])
-            nc.vector.scalar_tensor_tensor(
-                best[side][:], leaf[vector_leaf][:], bias[:], best[side][:], ADD, MAX
-            )
-        nc.vector.scalar_tensor_tensor(best["a"][:], left[:], bias3[:], best["a"][:], ADD, MAX)
-        nc.vector.tensor_tensor(best["a"][:], best["a"][:], best["b"][:], MAX)
+        first_leaf = work("first_leaf")
+        nc.scalar.copy(first_leaf[:], e3[:])
+        h1 = work("h1")
+        nc.vector.tensor_tensor(h1[:], e4[:], first_leaf[:], ADD)
+        best = work("best")
+        nc.vector.tensor_tensor(best[:], e4[:], first_leaf[:], MAX)
+        nc.vector.scalar_tensor_tensor(h1[:], e1[:], bias3[:], h1[:], ADD, ADD)
 
-        top = held.tile([P, TREES], F32, name="top")
+        above = work("above")
+        nc.vector.scalar_tensor_tensor(above[:], e0[:], bias[:], h1[:], ADD, ADD)
+        nc.scalar.activation(above[:], above[:], RELU)
+
+        nc.vector.scalar_tensor_tensor(best[:], best[:], bias[:], h1[:], ADD, MAX)
+        best_right = work("best_right")
+        nc.scalar.activation(best_right[:], e5[:], RELU, bias=bias[:])
+        nc.vector.scalar_tensor_tensor(best_right[:], e6[:], bias[:], best_right[:], ADD, MAX)
+        nc.vector.tensor_tensor(best[:], best[:], best_right[:], MAX)
+
+        top = work("top")
         nc.vector.scalar_tensor_tensor(top[:], right[:], bias3[:], above[:], ADD, ADD)
-        nc.vector.tensor_tensor(top[:], top[:], best["a"][:], MAX)
+        nc.vector.tensor_tensor(top[:], top[:], best[:], MAX)
         nc.sync.dma_start(out, top[:])

@@ -53,9 +53,9 @@ def tile_batchprogramclassifier_kernel(tc, table, w, b, offs, out):
                     )
             return bank
 
-        e3 = project_sum("e3", [3])
         e4 = project_sum("e4", [4])
-        e1 = project_sum("e1", [1])
+        e3 = project_sum("e3", [3])
+        e1_e3 = project_sum("e1_e3", [1, 3])
         e0 = project_sum("e0", [0])
         e5 = project_sum("e5", [5])
         e6 = project_sum("e6", [6])
@@ -64,13 +64,12 @@ def tile_batchprogramclassifier_kernel(tc, table, w, b, offs, out):
         def work(name):
             return held.tile([P, TREES], F32, name=name)
 
-        first_leaf = work("first_leaf")
-        nc.scalar.copy(first_leaf[:], e3[:])
-        h1 = work("h1")
-        nc.vector.tensor_tensor(h1[:], e4[:], first_leaf[:], ADD)
+        leaf4 = work("leaf4")
+        nc.scalar.copy(leaf4[:], e4[:])
         best = work("best")
-        nc.vector.tensor_tensor(best[:], e4[:], first_leaf[:], MAX)
-        nc.vector.scalar_tensor_tensor(h1[:], e1[:], bias3[:], h1[:], ADD, ADD)
+        nc.vector.tensor_tensor(best[:], e3[:], leaf4[:], MAX)
+        h1 = work("h1")
+        nc.vector.scalar_tensor_tensor(h1[:], e1_e3[:], bias3[:], leaf4[:], ADD, ADD)
 
         above = work("above")
         nc.vector.scalar_tensor_tensor(above[:], e0[:], bias[:], h1[:], ADD, ADD)

@@ -54,11 +54,11 @@ def tile_batchprogramclassifier_kernel(tc, table, w, b, offs, out):
             return bank
 
         e4 = project_sum("e4", [4])
-        e3 = project_sum("e3", [3])
         e1_e3 = project_sum("e1_e3", [1, 3])
         e0 = project_sum("e0", [0])
-        e5 = project_sum("e5", [5])
+        e3 = project_sum("e3", [3])
         e6 = project_sum("e6", [6])
+        e5 = project_sum("e5", [5])
         right = project_sum("right", [2, 5, 6])
 
         def work(name):
@@ -66,8 +66,6 @@ def tile_batchprogramclassifier_kernel(tc, table, w, b, offs, out):
 
         leaf4 = work("leaf4")
         nc.scalar.copy(leaf4[:], e4[:])
-        best = work("best")
-        nc.vector.tensor_tensor(best[:], e3[:], leaf4[:], MAX)
         h1 = work("h1")
         nc.vector.scalar_tensor_tensor(h1[:], e1_e3[:], bias3[:], leaf4[:], ADD, ADD)
 
@@ -75,10 +73,12 @@ def tile_batchprogramclassifier_kernel(tc, table, w, b, offs, out):
         nc.vector.scalar_tensor_tensor(above[:], e0[:], bias[:], h1[:], ADD, ADD)
         nc.scalar.activation(above[:], above[:], RELU)
 
+        best = work("best")
+        nc.vector.tensor_tensor(best[:], e3[:], leaf4[:], MAX)
         nc.vector.scalar_tensor_tensor(best[:], best[:], bias[:], h1[:], ADD, MAX)
         best_right = work("best_right")
-        nc.scalar.activation(best_right[:], e5[:], RELU, bias=bias[:])
-        nc.vector.scalar_tensor_tensor(best_right[:], e6[:], bias[:], best_right[:], ADD, MAX)
+        nc.scalar.activation(best_right[:], e6[:], RELU, bias=bias[:])
+        nc.vector.scalar_tensor_tensor(best_right[:], e5[:], bias[:], best_right[:], ADD, MAX)
         nc.vector.tensor_tensor(best[:], best[:], best_right[:], MAX)
 
         top = work("top")

@@ -71,7 +71,6 @@ def tile_batchprogramclassifier_kernel(tc, table, w, b, offs, out):
 
         above = work("above")
         nc.vector.scalar_tensor_tensor(above[:], e0[:], bias[:], h1[:], ADD, ADD)
-        nc.scalar.activation(above[:], above[:], RELU)
 
         best = work("best")
         nc.vector.tensor_tensor(best[:], e3[:], leaf4[:], MAX)
@@ -82,6 +81,6 @@ def tile_batchprogramclassifier_kernel(tc, table, w, b, offs, out):
         nc.vector.tensor_tensor(best[:], best[:], best_right[:], MAX)
 
         top = work("top")
-        nc.vector.scalar_tensor_tensor(top[:], right[:], bias3[:], above[:], ADD, ADD)
-        nc.vector.tensor_tensor(top[:], top[:], best[:], MAX)
+        nc.vector.scalar_tensor_tensor(top[:], above[:], 0.0, right[:], MAX, ADD)
+        nc.vector.scalar_tensor_tensor(top[:], top[:], bias3[:], best[:], ADD, MAX)
         nc.sync.dma_start(out, top[:])

@@ -7,6 +7,7 @@ RELU = mybir.ActivationFunctionType.Relu
 P = 128
 WORDS = 256
 TREES = 256
+HALF = TREES // 2
 NODES = 7
 PIECE_COLS = TREES // 16
 
@@ -36,30 +37,28 @@ def tile_batchprogramclassifier_kernel(tc, table, w, b, offs, out):
         bias3 = held.tile([P, 1], F32, name="bias3")
         nc.vector.tensor_scalar(bias3[:], bias[:], 3.0, None, MULT)
 
-        def project_sum(name, nodes):
-            bank = psum.tile([P, TREES], F32, name=name)
+        def project_sum(name, nodes, lo=0, hi=TREES):
+            bank = psum.tile([P, hi - lo], F32, name=name)
             for n in nodes:
                 first, last = n == nodes[0], n == nodes[-1]
-                cuts = 1 if first or last else 2
-                width = TREES // cuts
-                for c in range(cuts):
-                    col = n * PIECE_COLS + c * (width // 16)
-                    nc.tensor.matmul(
-                        bank[:, c * width : (c + 1) * width],
-                        weights[:],
-                        words[:].indirect(offsets[:, col : col + width // 16]),
-                        start=first,
-                        stop=last,
-                    )
+                nc.tensor.matmul(
+                    bank[:, : hi - lo],
+                    weights[:],
+                    words[:].indirect(offsets[:, n * PIECE_COLS + lo // 16 : n * PIECE_COLS + hi // 16]),
+                    start=first,
+                    stop=last,
+                )
             return bank
 
         e4 = project_sum("e4", [4])
         e1_e3 = project_sum("e1_e3", [1, 3])
-        e0 = project_sum("e0", [0])
         e3 = project_sum("e3", [3])
         e6 = project_sum("e6", [6])
+        e0 = project_sum("e0", [0])
         e5 = project_sum("e5", [5])
-        right = project_sum("right", [2, 5, 6])
+        right = [
+            project_sum(f"right{half}", [2, 5, 6], half * HALF, (half + 1) * HALF) for half in range(2)
+        ]
 
         def work(name):
             return held.tile([P, TREES], F32, name=name)
@@ -81,6 +80,10 @@ def tile_batchprogramclassifier_kernel(tc, table, w, b, offs, out):
         nc.vector.tensor_tensor(best[:], best[:], best_right[:], MAX)
 
         top = work("top")
-        nc.vector.scalar_tensor_tensor(top[:], above[:], 0.0, right[:], MAX, ADD)
-        nc.vector.scalar_tensor_tensor(top[:], top[:], bias3[:], best[:], ADD, MAX)
+        for half in range(2):
+            part = slice(half * HALF, (half + 1) * HALF)
+            nc.vector.scalar_tensor_tensor(top[:, part], above[:, part], 0.0, right[half][:], MAX, ADD)
+        for half in range(2):
+            part = slice(half * HALF, (half + 1) * HALF)
+            nc.vector.scalar_tensor_tensor(top[:, part], top[:, part], bias3[:], best[:, part], ADD, MAX)
         nc.sync.dma_start(out, top[:])

@@ -51,11 +51,11 @@ def tile_batchprogramclassifier_kernel(tc, table, w, b, offs, out):
             return bank
 
         e4 = project_sum("e4", [4])
-        e1_e3 = project_sum("e1_e3", [1, 3])
-        e3 = project_sum("e3", [3])
         e6 = project_sum("e6", [6])
-        e0 = project_sum("e0", [0])
+        e3 = project_sum("e3", [3])
+        e1_e3 = project_sum("e1_e3", [1, 3])
         e5 = project_sum("e5", [5])
+        e0 = project_sum("e0", [0])
         right = [
             project_sum(f"right{half}", [2, 5, 6], half * HALF, (half + 1) * HALF) for half in range(2)
         ]
@@ -65,18 +65,19 @@ def tile_batchprogramclassifier_kernel(tc, table, w, b, offs, out):
 
         leaf4 = work("leaf4")
         nc.scalar.copy(leaf4[:], e4[:])
-        h1 = work("h1")
-        nc.vector.scalar_tensor_tensor(h1[:], e1_e3[:], bias3[:], leaf4[:], ADD, ADD)
-
-        above = work("above")
-        nc.vector.scalar_tensor_tensor(above[:], e0[:], bias[:], h1[:], ADD, ADD)
+        leaf6 = work("leaf6")
+        nc.scalar.activation(leaf6[:], e6[:], RELU, bias=bias[:])
 
         best = work("best")
         nc.vector.tensor_tensor(best[:], e3[:], leaf4[:], MAX)
-        nc.vector.scalar_tensor_tensor(best[:], best[:], bias[:], h1[:], ADD, MAX)
+        h1 = work("h1")
+        nc.vector.scalar_tensor_tensor(h1[:], e1_e3[:], bias3[:], leaf4[:], ADD, ADD)
         best_right = work("best_right")
-        nc.scalar.activation(best_right[:], e6[:], RELU, bias=bias[:])
-        nc.vector.scalar_tensor_tensor(best_right[:], e5[:], bias[:], best_right[:], ADD, MAX)
+        nc.vector.scalar_tensor_tensor(best_right[:], e5[:], bias[:], leaf6[:], ADD, MAX)
+        nc.vector.scalar_tensor_tensor(best[:], best[:], bias[:], h1[:], ADD, MAX)
+
+        above = work("above")
+        nc.vector.scalar_tensor_tensor(above[:], e0[:], bias[:], h1[:], ADD, ADD)
         nc.vector.tensor_tensor(best[:], best[:], best_right[:], MAX)
 
         top = work("top")

import concourse.mybir as mybir

BF16, F32, U16 = mybir.dt.bfloat16, mybir.dt.float32, mybir.dt.uint16
ADD, MAX, MULT = mybir.AluOpType.add, mybir.AluOpType.max, mybir.AluOpType.mult
RELU = mybir.ActivationFunctionType.Relu

P = 128
WORDS = 256
TREES = 256
HALF = TREES // 2
NODES = 7
PIECE_COLS = TREES // 16

FLOPS = 2 * P * P * NODES * TREES


def tile_batchprogramclassifier_kernel(tc, table, w, b, offs, out):
    nc = tc.nc
    with (
        tc.tile_pool(name="held", bufs=1) as held,
        tc.psum_pool(name="psum", bufs=1) as psum,
    ):
        offsets = held.tile([P, NODES * PIECE_COLS], U16, name="offsets")
        nc.sync.dma_start(offsets[:], offs)
        words = held.tile([P, WORDS], BF16, name="words")
        nc.scalar.dma_start(words[:], table)
        weights = held.tile([P, P], BF16, name="weights")
        nc.sync.dma_start(weights[:], w)
        bias = held.tile([P, 1], F32, name="bias")
        nc.scalar.dma_start(bias[:], b)

        zeros = held.tile([P, 1], F32, name="zeros")
        nc.vector.memset(zeros[:], 0.0)
        table_loaded = held.tile([P, 1], F32, name="table_loaded")
        nc.scalar.activation(table_loaded[:], zeros[:], RELU)

        bias3 = held.tile([P, 1], F32, name="bias3")
        nc.vector.tensor_scalar(bias3[:], bias[:], 3.0, None, MULT)

        def project_sum(name, nodes, lo=0, hi=TREES):
            bank = psum.tile([P, hi - lo], F32, name=name)
            for n in nodes:
                first, last = n == nodes[0], n == nodes[-1]
                nc.tensor.matmul(
                    bank[:, : hi - lo],
                    weights[:],
                    words[:].indirect(offsets[:, n * PIECE_COLS + lo // 16 : n * PIECE_COLS + hi // 16]),
                    start=first,
                    stop=last,
                )
            return bank

        e4 = project_sum("e4", [4])
        e6 = project_sum("e6", [6])
        e3 = project_sum("e3", [3])
        e1_e3 = project_sum("e1_e3", [1, 3])
        e5 = project_sum("e5", [5])
        e0 = project_sum("e0", [0])
        right = [
            project_sum(f"right{half}", [2, 5, 6], half * HALF, (half + 1) * HALF) for half in range(2)
        ]

        def work(name):
            return held.tile([P, TREES], F32, name=name)

        leaf4 = work("leaf4")
        nc.scalar.copy(leaf4[:], e4[:])
        leaf6 = work("leaf6")
        nc.scalar.activation(leaf6[:], e6[:], RELU, bias=bias[:])

        best = work("best")
        nc.vector.tensor_tensor(best[:], e3[:], leaf4[:], MAX)
        h1 = work("h1")
        nc.vector.scalar_tensor_tensor(h1[:], e1_e3[:], bias3[:], leaf4[:], ADD, ADD)
        best_right = work("best_right")
        nc.vector.scalar_tensor_tensor(best_right[:], e5[:], bias[:], leaf6[:], ADD, MAX)
        nc.vector.scalar_tensor_tensor(best[:], best[:], bias[:], h1[:], ADD, MAX)

        above = work("above")
        nc.vector.scalar_tensor_tensor(above[:], e0[:], bias[:], h1[:], ADD, ADD)
        nc.vector.tensor_tensor(best[:], best[:], best_right[:], MAX)

        top = work("top")
        for half in range(2):
            part = slice(half * HALF, (half + 1) * HALF)
            nc.vector.scalar_tensor_tensor(top[:, part], above[:, part], 0.0, right[half][:], MAX, ADD)
        for half in range(2):
            part = slice(half * HALF, (half + 1) * HALF)
            nc.vector.scalar_tensor_tensor(top[:, part], top[:, part], bias3[:], best[:, part], ADD, MAX)
        nc.sync.dma_start(out, top[:])
